import numpy as np
import ml_dtypes


def mxq(x, axis, fmt="e4m3"):
    dtype, down = {"e4m3": (ml_dtypes.float8_e4m3fn, 7), "e5m2": (ml_dtypes.float8_e5m2, 14)}[fmt]
    v = np.moveaxis(np.asarray(x, np.float32).astype(ml_dtypes.bfloat16).astype(np.float64), axis, -1)
    blocks = v.reshape(v.shape[:-1] + (-1, 32))
    amax = np.abs(blocks).max(-1, keepdims=True)
    byte = np.maximum(np.where(amax > 0, np.frexp(amax)[1] - 1 + 127, 0) - down, 1)
    scale = np.exp2(byte - 127.0)
    codes = (blocks / scale).astype(np.float32).astype(dtype).astype(np.float64)
    return np.moveaxis((codes * scale).reshape(v.shape), -1, axis)


WIDE = False


def mx_kscale(k):
    if not WIDE:
        return np.ones(k)
    levels = np.array([10, -10, 5, -5, 0])
    a = np.random.permutation(np.resize(levels, k // 512 * 4)).reshape(k // 512, 4)
    idx = np.arange(k)
    return np.exp2(a[idx // 512, idx % 128 // 32])


BF16 = ml_dtypes.bfloat16


def bf(x):
    return np.asarray(x, np.float32).astype(BF16)


def f64(x):
    return np.asarray(x).astype(np.float64)


E2M1 = np.array([0.0, 0.5, 1.0, 1.5, 2.0, 3.0, 4.0, 6.0, -0.0, -0.5, -1.0, -1.5, -2.0, -3.0, -4.0, -6.0])


def pack_weight(w, fmt):
    k, n = w.shape
    w = f64(bf(w)).reshape(k // 32, 32, n)
    amax = np.abs(w).max(1)
    if fmt == "e4m3":
        byte = np.frexp(amax)[1] - 1 + 127 - 7
    else:
        mant, ex = np.frexp(amax / 6.0)
        byte = np.where(mant > 0.5, ex, ex - 1) + 127
    byte = np.clip(np.where(amax > 0, byte, 1), 1, 254)
    scaled = (w * np.exp2(127.0 - byte)[:, None, :]).reshape(k, n).astype(np.float32)
    by_word = np.ascontiguousarray(scaled.reshape(k // 512, 128, 4, n).transpose(0, 1, 3, 2))
    if fmt == "e4m3":
        words = by_word.astype(ml_dtypes.float8_e4m3fn).view(np.uint8)
    else:
        c = by_word.astype(ml_dtypes.float4_e2m1fn).view(np.uint8) & 0xF
        words = c[..., 0::2] | (c[..., 1::2] << 4)
    return np.ascontiguousarray(words), np.ascontiguousarray(byte.astype(np.uint8).reshape(k // 512, 16, n))


def unpack_weight(words, scales, fmt):
    g, p, n, _ = words.shape
    if fmt == "e4m3":
        vals = np.ascontiguousarray(words).view(ml_dtypes.float8_e4m3fn).astype(np.float64)
    else:
        nib = np.empty((g, p, n, 4), np.uint8)
        nib[..., 0::2] = words & 0xF
        nib[..., 1::2] = words >> 4
        vals = E2M1[nib]
    vals = vals * np.repeat(np.exp2(scales.astype(np.float64) - 127.0), 8, axis=1)[..., None]
    return vals.transpose(0, 1, 3, 2).reshape(g * 512, n)

def pack4(w):
    words, scales = pack_weight(w, "e2m1")
    return words.reshape(words.shape[0], 128, -1), scales


def unpack4(words, scales):
    return unpack_weight(words.reshape(words.shape[0], 128, -1, 2), scales, "e2m1")


T, B, D, U, V, E = 3, 4096, 512, 1024, 16, 8
G = 2 * E


def softmax(v):
    e = np.exp(v - v.max(-1, keepdims=True))
    return e / e.sum(-1, keepdims=True)


def setup_inputs():
    rn = np.random.standard_normal
    s = mx_kscale(U)
    task_h = bf(np.abs(rn((T, B, U))) * 0.55 * s)
    share_h = bf(np.abs(rn((B, U))) * 0.5 * s)
    ews1 = rn((U, V, E)) * 2.0 / np.sqrt(U) / s[:, None, None]
    ews1_words, ews1_scales = pack4(ews1.reshape(U, V * E))
    ebs1 = bf(rn((V, E)) * 0.5)
    ew1 = rn((T, U, V, E)) * 2.0 / np.sqrt(U) / s[None, :, None, None]
    ew1_words, ew1_scales = pack4(ew1.reshape(T, U, V * E).reshape(-1, V * E))
    eb1 = bf(rn((T, V, E)) * 0.5)
    gate_pre1 = bf(rn((T, B, G)))
    gb1 = bf(rn((T, G)) * 0.5)
    return {
        "task_h": task_h,
        "share_h": share_h,
        "ews1_words": ews1_words,
        "ews1_scales": ews1_scales,
        "ebs1": ebs1,
        "ew1_words": ew1_words,
        "ew1_scales": ew1_scales,
        "eb1": eb1,
        "gate_pre1": gate_pre1,
        "gb1": gb1,
    }


def reference(task_h, share_h, ews1_words, ews1_scales, ebs1, ew1_words, ew1_scales, eb1, gate_pre1, gb1):
    es = np.maximum((mxq(f64(share_h), 1, "e4m3") @ unpack4(ews1_words, ews1_scales)).reshape(B, V, E) + f64(ebs1), 0.0)
    et = np.maximum((mxq(f64(task_h), 2, "e4m3") @ unpack4(ew1_words, ew1_scales).reshape(T, U, V * E)).reshape(T, B, V, E) + f64(eb1)[:, None], 0.0)
    g = softmax(f64(gate_pre1) + f64(gb1)[:, None])
    comb = np.concatenate([et, np.broadcast_to(es, et.shape)], axis=-1)
    return (comb * g[:, :, None, :]).sum(-1)

@@ -1,0 +1,220 @@
+from contextlib import ExitStack
+
+import concourse.mybir as mybir
+from concourse.masks import make_identity
+
+F32 = mybir.dt.float32
+BF16 = mybir.dt.bfloat16
+I32 = mybir.dt.int32
+U32 = mybir.dt.uint32
+U8 = mybir.dt.uint8
+FP8X4 = mybir.dt.float8_e4m3fn_x4
+FP4X4 = mybir.dt.float4_e2m1fn_x4
+ALU = mybir.AluOpType
+ACT = mybir.ActivationFunctionType
+AXIS = mybir.AxisListType
+
+P = 128
+TASKS = 3
+STREAMS = TASKS + 1
+BATCH = 4096
+FEATURES = 1024
+UNITS = 16
+EXPERTS = 8
+GATES = 2 * EXPERTS
+COLS = UNITS * EXPERTS
+PACK = 4
+K_PASS = P * PACK
+PASSES = FEATURES // K_PASS
+PAIRS = PACK // 2
+ROW_TILES = BATCH // P
+STORE_TILES = 8
+X_BUFS = 6
+
+FLOPS = 2 * STREAMS * BATCH * FEATURES * COLS
+
+
+def tile_plelayer_pb_t_e_kernel(
+    tc, task_h, share_h, ews1_words, ews1_scales, ebs1, ew1_words, ew1_scales, eb1, gate_pre1, gb1, out
+):
+    nc = tc.nc
+    with ExitStack() as ctx:
+        const = ctx.enter_context(tc.tile_pool(name="const", bufs=1))
+        x_pool = ctx.enter_context(tc.tile_pool(name="x", bufs=X_BUFS))
+        work = ctx.enter_context(tc.tile_pool(name="work", bufs=2))
+        turned_pool = ctx.enter_context(tc.psum_pool(name="turned", bufs=6))
+        acc_pool = ctx.enter_context(tc.psum_pool(name="acc", bufs=2))
+        ctx.enter_context(tc.manual_schedule())
+
+        task_rows = task_h.rearrange("t (p j) k -> p t j k", j=ROW_TILES)
+        share_rows = share_h.rearrange("(p j) k -> p j k", j=ROW_TILES)
+        out_rows = out.rearrange("t (p j) v -> p t j v", j=ROW_TILES)
+
+        w_words = const.tile([P, STREAMS * PASSES, 2 * COLS], U8, align_bytes=64)
+        w_planes = const.tile([P, STREAMS * PASSES, COLS], U8, align_bytes=64)
+        own_passes = TASKS * PASSES
+        nc.vector.memset(w_planes[:].bitcast(I32), 0)
+        nc.sync.dma_start(
+            out=w_words[:, 0:own_passes, :].bitcast(I32), in_=ew1_words.rearrange("g p n -> p g n").bitcast(I32)
+        )
+        nc.sync.dma_start(
+            out=w_words[:, own_passes:, :].bitcast(I32), in_=ews1_words.rearrange("g p n -> p g n").bitcast(I32)
+        )
+        for quad in range(4):
+            rows = slice(4 * quad, 4 * quad + 4)
+            parts = slice(32 * quad, 32 * quad + 4)
+            nc.sync.dma_start(
+                out=w_planes[parts, 0:own_passes, :].bitcast(I32),
+                in_=ew1_scales[:, rows, :].rearrange("g r n -> r g n").bitcast(I32),
+            )
+            nc.sync.dma_start(
+                out=w_planes[parts, own_passes:, :].bitcast(I32),
+                in_=ews1_scales[:, rows, :].rearrange("g r n -> r g n").bitcast(I32),
+            )
+
+        def load_row_tile(j):
+            x_tile = x_pool.tile([P, STREAMS, FEATURES], BF16)
+            nc.sync.dma_start(out=x_tile[:, 0:TASKS, :], in_=task_rows[:, :, j, :])
+            nc.sync.dma_start(out=x_tile[:, TASKS, :], in_=share_rows[:, j, :])
+            return x_tile
+
+        x_tiles = {}
+        for j in range(X_BUFS):
+            x_tiles[j] = load_row_tile(j)
+
+        ident = const.tile([P, P], F32)
+        make_identity(nc, ident[:])
+
+        gate_bf = const.tile([P, TASKS, ROW_TILES, GATES], BF16)
+        nc.scalar.dma_start(out=gate_bf[:], in_=gate_pre1.rearrange("t (p j) i -> p t j i", j=ROW_TILES))
+        gb_bf = const.tile([P, TASKS, GATES], BF16)
+        nc.scalar.dma_start(
+            out=gb_bf[:].rearrange("p t i -> p (t i)"), in_=gb1.rearrange("t i -> (t i)").partition_broadcast(P)
+        )
+        bias_bf = const.tile([P, STREAMS * COLS], BF16)
+        nc.scalar.dma_start(
+            out=bias_bf[:, 0 : TASKS * COLS], in_=eb1.rearrange("t v e -> (t v e)").partition_broadcast(P)
+        )
+        nc.scalar.dma_start(
+            out=bias_bf[:, TASKS * COLS :], in_=ebs1.rearrange("v e -> (v e)").partition_broadcast(P)
+        )
+
+        rows_all = TASKS * ROW_TILES
+        logits = const.tile([P, TASKS, ROW_TILES, GATES], F32)
+        nc.vector.tensor_tensor(
+            out=logits[:],
+            in0=gate_bf[:],
+            in1=gb_bf[:].unsqueeze(2).to_broadcast([P, TASKS, ROW_TILES, GATES]),
+            op=ALU.add,
+        )
+        logits_flat = logits[:].rearrange("p t j i -> p (t j) i")
+        top = const.tile([P, rows_all], F32)
+        nc.vector.tensor_reduce(out=top[:], in_=logits_flat, axis=AXIS.X, op=ALU.max)
+        shifted = const.tile([P, rows_all, GATES], F32)
+        nc.vector.tensor_tensor(
+            out=shifted[:], in0=logits_flat, in1=top[:].unsqueeze(2).to_broadcast([P, rows_all, GATES]), op=ALU.subtract
+        )
+        expo = const.tile([P, rows_all, GATES], F32)
+        nc.scalar.activation(out=expo[:], in_=shifted[:], func=ACT.Exp)
+        total = const.tile([P, rows_all], F32)
+        nc.vector.tensor_reduce(out=total[:], in_=expo[:], axis=AXIS.X, op=ALU.add)
+        inverse = const.tile([P, rows_all], F32)
+        nc.vector.reciprocal(out=inverse[:], in_=total[:])
+        gates = const.tile([P, TASKS, ROW_TILES, GATES], F32)
+        nc.vector.tensor_tensor(
+            out=gates[:].rearrange("p t j i -> p (t j) i"),
+            in0=expo[:],
+            in1=inverse[:].unsqueeze(2).to_broadcast([P, rows_all, GATES]),
+            op=ALU.mult,
+        )
+
+        bias = const.tile([P, STREAMS * COLS], F32)
+        nc.vector.tensor_copy(out=bias[:], in_=bias_bf[:])
+        result = const.tile([P, TASKS, ROW_TILES, UNITS], F32)
+
+        def transpose_row_tile(x_tile):
+            grouped = work.tile([P, STREAMS, PASSES, P, PACK], BF16, align_bytes=64)
+            for s in range(STREAMS):
+                words = x_tile[:, s, :].bitcast(F32)
+                turned = turned_pool.tile([P, PASSES, PAIRS, P], F32)
+                for g in range(PASSES):
+                    first = g * P * PAIRS
+                    for u in range(PAIRS):
+                        nc.tensor.transpose(
+                            turned[:, g, u, :], words[:, first + u : first + P * PAIRS : PAIRS], ident[:]
+                        )
+                nc.scalar.copy(out=grouped[:, s].bitcast(F32), in_=turned[:].rearrange("p g u r -> p g r u"))
+            return grouped
+
+        def quantise_row_tile(grouped):
+            codes = work.tile([P, STREAMS * PASSES * P], U32, align_bytes=64)
+            x_scales = work.tile([P, STREAMS * PASSES * P], U8, align_bytes=64)
+            nc.vector.quantize_mx(
+                out=codes[:].bitcast(FP8X4), scales=x_scales[:], in_=grouped[:].rearrange("p s g r t -> p (s g r t)")
+            )
+            return codes, x_scales
+
+        def expert_matmuls(codes, x_scales):
+            acc = acc_pool.tile([P, STREAMS, COLS], F32)
+            for s in range(STREAMS):
+                for g in range(PASSES):
+                    w = s * PASSES + g
+                    rows = slice(w * P, (w + 1) * P)
+                    nc.tensor.matmul_mx(
+                        out=acc[:, s, :],
+                        lhsT=codes[:, rows].bitcast(FP8X4),
+                        lhsT_scale=x_scales[:, rows],
+                        rhs=w_words[:, w, :].bitcast(FP4X4),
+                        rhs_scale=w_planes[:, w, :],
+                        start=(g == 0),
+                        stop=(g == PASSES - 1),
+                    )
+            return acc
+
+        def bias_relu(acc):
+            pre = work.tile([P, STREAMS * COLS], F32)
+            nc.vector.tensor_tensor(out=pre[:], in0=acc[:].rearrange("p s n -> p (s n)"), in1=bias[:], op=ALU.add)
+            act = work.tile([P, STREAMS, UNITS, EXPERTS], F32)
+            nc.scalar.activation(out=act[:].rearrange("p s v e -> p (s v e)"), in_=pre[:], func=ACT.Relu)
+            return act
+
+        def combine(act, j):
+            shape = [P, TASKS, UNITS, EXPERTS]
+            prod = work.tile([P, TASKS, UNITS, GATES], F32)
+            nc.vector.tensor_tensor(
+                out=prod[:, :, :, 0:EXPERTS],
+                in0=act[:, 0:TASKS],
+                in1=gates[:, :, j, 0:EXPERTS].unsqueeze(2).to_broadcast(shape),
+                op=ALU.mult,
+            )
+            nc.vector.tensor_tensor(
+                out=prod[:, :, :, EXPERTS:GATES],
+                in0=act[:, TASKS].unsqueeze(1).to_broadcast(shape),
+                in1=gates[:, :, j, EXPERTS:GATES].unsqueeze(2).to_broadcast(shape),
+                op=ALU.mult,
+            )
+            nc.vector.tensor_reduce(out=result[:, :, j, :], in_=prod[:], axis=AXIS.X, op=ALU.add)
+
+        grouped_of = {}
+        quantised_of = {}
+        acc_of = {}
+        act_of = {}
+        for step in range(ROW_TILES + 3):
+            if step < ROW_TILES:
+                grouped_of[step] = transpose_row_tile(x_tiles[step])
+                if step + X_BUFS < ROW_TILES:
+                    x_tiles[step + X_BUFS] = load_row_tile(step + X_BUFS)
+            if 0 <= step - 1 < ROW_TILES:
+                codes, x_scales = quantised_of[step - 1]
+                acc_of[step - 1] = expert_matmuls(codes, x_scales)
+            if 0 <= step - 2 < ROW_TILES:
+                act_of[step - 2] = bias_relu(acc_of[step - 2])
+            if 0 <= step - 3 < ROW_TILES:
+                j = step - 3
+                combine(act_of[j], j)
+                if (j + 1) % STORE_TILES == 0:
+                    done = slice(j + 1 - STORE_TILES, j + 1)
+                    queue = nc.sync if j + 1 == ROW_TILES else nc.gpsimd
+                    queue.dma_start(out=out_rows[:, :, done, :], in_=result[:, :, done, :])
+            if step < ROW_TILES:
+                quantised_of[step] = quantise_row_tile(grouped_of[step])

@@ -41,7 +41,7 @@ def tile_plelayer_pb_t_e_kernel(
     with ExitStack() as ctx:
         const = ctx.enter_context(tc.tile_pool(name="const", bufs=1))
         x_pool = ctx.enter_context(tc.tile_pool(name="x", bufs=X_BUFS))
-        work = ctx.enter_context(tc.tile_pool(name="work", bufs=2))
+        work = ctx.enter_context(tc.tile_pool(name="work", bufs=3))
         turned_pool = ctx.enter_context(tc.psum_pool(name="turned", bufs=6))
         acc_pool = ctx.enter_context(tc.psum_pool(name="acc", bufs=2))
         ctx.enter_context(tc.manual_schedule())
@@ -49,6 +49,14 @@ def tile_plelayer_pb_t_e_kernel(
         task_rows = task_h.rearrange("t (p j) k -> p t j k", j=ROW_TILES)
         share_rows = share_h.rearrange("(p j) k -> p j k", j=ROW_TILES)
         out_rows = out.rearrange("t (p j) v -> p t j v", j=ROW_TILES)
+
+        def load_row_tile(j):
+            x_tile = x_pool.tile([P, STREAMS, FEATURES], BF16)
+            nc.sync.dma_start(out=x_tile[:, 0:TASKS, :], in_=task_rows[:, :, j, :])
+            nc.sync.dma_start(out=x_tile[:, TASKS, :], in_=share_rows[:, j, :])
+            return x_tile
+
+        x_tiles = {0: load_row_tile(0)}
 
         w_words = const.tile([P, STREAMS * PASSES, 2 * COLS], U8, align_bytes=64)
         w_planes = const.tile([P, STREAMS * PASSES, COLS], U8, align_bytes=64)
@@ -72,14 +80,7 @@ def tile_plelayer_pb_t_e_kernel(
                 in_=ews1_scales[:, rows, :].rearrange("g r n -> r g n").bitcast(I32),
             )
 
-        def load_row_tile(j):
-            x_tile = x_pool.tile([P, STREAMS, FEATURES], BF16)
-            nc.sync.dma_start(out=x_tile[:, 0:TASKS, :], in_=task_rows[:, :, j, :])
-            nc.sync.dma_start(out=x_tile[:, TASKS, :], in_=share_rows[:, j, :])
-            return x_tile
-
-        x_tiles = {}
-        for j in range(X_BUFS):
+        for j in range(1, X_BUFS):
             x_tiles[j] = load_row_tile(j)
 
         ident = const.tile([P, P], F32)
@@ -114,19 +115,21 @@ def tile_plelayer_pb_t_e_kernel(
         nc.vector.tensor_tensor(
             out=shifted[:], in0=logits_flat, in1=top[:].unsqueeze(2).to_broadcast([P, rows_all, GATES]), op=ALU.subtract
         )
-        expo = const.tile([P, rows_all, GATES], F32)
-        nc.scalar.activation(out=expo[:], in_=shifted[:], func=ACT.Exp)
-        total = const.tile([P, rows_all], F32)
-        nc.vector.tensor_reduce(out=total[:], in_=expo[:], axis=AXIS.X, op=ALU.add)
-        inverse = const.tile([P, rows_all], F32)
-        nc.vector.reciprocal(out=inverse[:], in_=total[:])
         gates = const.tile([P, TASKS, ROW_TILES, GATES], F32)
-        nc.vector.tensor_tensor(
-            out=gates[:].rearrange("p t j i -> p (t j) i"),
-            in0=expo[:],
-            in1=inverse[:].unsqueeze(2).to_broadcast([P, rows_all, GATES]),
-            op=ALU.mult,
-        )
+
+        def normalise_gates():
+            expo = const.tile([P, rows_all, GATES], F32)
+            nc.scalar.activation(out=expo[:], in_=shifted[:], func=ACT.Exp)
+            total = const.tile([P, rows_all], F32)
+            nc.vector.tensor_reduce(out=total[:], in_=expo[:], axis=AXIS.X, op=ALU.add)
+            inverse = const.tile([P, rows_all], F32)
+            nc.vector.reciprocal(out=inverse[:], in_=total[:])
+            nc.gpsimd.tensor_tensor(
+                out=gates[:].rearrange("p t j i -> p (t j) i"),
+                in0=expo[:],
+                in1=inverse[:].unsqueeze(2).to_broadcast([P, rows_all, GATES]),
+                op=ALU.mult,
+            )
 
         bias = const.tile([P, STREAMS * COLS], F32)
         nc.vector.tensor_copy(out=bias[:], in_=bias_bf[:])
@@ -178,28 +181,32 @@ def tile_plelayer_pb_t_e_kernel(
             nc.scalar.activation(out=act[:].rearrange("p s v e -> p (s v e)"), in_=pre[:], func=ACT.Relu)
             return act
 
-        def combine(act, j):
+        def weigh(act, j):
             shape = [P, TASKS, UNITS, EXPERTS]
             prod = work.tile([P, TASKS, UNITS, GATES], F32)
-            nc.vector.tensor_tensor(
+            nc.gpsimd.tensor_tensor(
                 out=prod[:, :, :, 0:EXPERTS],
                 in0=act[:, 0:TASKS],
                 in1=gates[:, :, j, 0:EXPERTS].unsqueeze(2).to_broadcast(shape),
                 op=ALU.mult,
             )
-            nc.vector.tensor_tensor(
+            nc.gpsimd.tensor_tensor(
                 out=prod[:, :, :, EXPERTS:GATES],
                 in0=act[:, TASKS].unsqueeze(1).to_broadcast(shape),
                 in1=gates[:, :, j, EXPERTS:GATES].unsqueeze(2).to_broadcast(shape),
                 op=ALU.mult,
             )
+            return prod
+
+        def sum_experts(prod, j):
             nc.vector.tensor_reduce(out=result[:, :, j, :], in_=prod[:], axis=AXIS.X, op=ALU.add)
 
         grouped_of = {}
         quantised_of = {}
         acc_of = {}
         act_of = {}
-        for step in range(ROW_TILES + 3):
+        prod_of = {}
+        for step in range(ROW_TILES + 4):
             if step < ROW_TILES:
                 grouped_of[step] = transpose_row_tile(x_tiles[step])
                 if step + X_BUFS < ROW_TILES:
@@ -210,11 +217,14 @@ def tile_plelayer_pb_t_e_kernel(
             if 0 <= step - 2 < ROW_TILES:
                 act_of[step - 2] = bias_relu(acc_of[step - 2])
             if 0 <= step - 3 < ROW_TILES:
-                j = step - 3
-                combine(act_of[j], j)
+                prod_of[step - 3] = weigh(act_of[step - 3], step - 3)
+            if 0 <= step - 4 < ROW_TILES:
+                j = step - 4
+                sum_experts(prod_of[j], j)
                 if (j + 1) % STORE_TILES == 0:
                     done = slice(j + 1 - STORE_TILES, j + 1)
-                    queue = nc.sync if j + 1 == ROW_TILES else nc.gpsimd
-                    queue.dma_start(out=out_rows[:, :, done, :], in_=result[:, :, done, :])
+                    nc.sync.dma_start(out=out_rows[:, :, done, :], in_=result[:, :, done, :])
             if step < ROW_TILES:
                 quantised_of[step] = quantise_row_tile(grouped_of[step])
+            if step == 0:
+                normalise_gates()

@@ -30,6 +30,7 @@ PAIRS = PACK // 2
 ROW_TILES = BATCH // P
 STORE_TILES = 8
 X_BUFS = 6
+VECTOR_TILES = 2
 
 FLOPS = 2 * STREAMS * BATCH * FEATURES * COLS
 
@@ -174,9 +175,12 @@ def tile_plelayer_pb_t_e_kernel(
                     )
             return acc
 
-        def bias_relu(acc):
+        def add_bias(acc):
             pre = work.tile([P, STREAMS * COLS], F32)
             nc.vector.tensor_tensor(out=pre[:], in0=acc[:].rearrange("p s n -> p (s n)"), in1=bias[:], op=ALU.add)
+            return pre
+
+        def relu(pre):
             act = work.tile([P, STREAMS, UNITS, EXPERTS], F32)
             nc.scalar.activation(out=act[:].rearrange("p s v e -> p (s v e)"), in_=pre[:], func=ACT.Relu)
             return act
@@ -198,12 +202,27 @@ def tile_plelayer_pb_t_e_kernel(
             )
             return prod
 
+        def weigh_on_vector(pre, j):
+            prod = work.tile([P, TASKS, UNITS, GATES], F32)
+            for t in range(TASKS):
+                for s, first in ((t, 0), (TASKS, EXPERTS)):
+                    nc.vector.scalar_tensor_tensor(
+                        out=prod[:, t, :, first : first + EXPERTS],
+                        in0=pre[:, s * COLS : (s + 1) * COLS].rearrange("p (v e) -> p v e", e=EXPERTS),
+                        scalar=0.0,
+                        in1=gates[:, t, j, first : first + EXPERTS].unsqueeze(1).to_broadcast([P, UNITS, EXPERTS]),
+                        op0=ALU.max,
+                        op1=ALU.mult,
+                    )
+            return prod
+
         def sum_experts(prod, j):
             nc.vector.tensor_reduce(out=result[:, :, j, :], in_=prod[:], axis=AXIS.X, op=ALU.add)
 
         grouped_of = {}
         quantised_of = {}
         acc_of = {}
+        pre_of = {}
         act_of = {}
         prod_of = {}
         for step in range(ROW_TILES + 4):
@@ -215,9 +234,13 @@ def tile_plelayer_pb_t_e_kernel(
                 codes, x_scales = quantised_of[step - 1]
                 acc_of[step - 1] = expert_matmuls(codes, x_scales)
             if 0 <= step - 2 < ROW_TILES:
-                act_of[step - 2] = bias_relu(acc_of[step - 2])
-            if 0 <= step - 3 < ROW_TILES:
+                pre_of[step - 2] = add_bias(acc_of[step - 2])
+                if step - 2 < ROW_TILES - VECTOR_TILES:
+                    act_of[step - 2] = relu(pre_of[step - 2])
+            if 0 <= step - 3 < ROW_TILES - VECTOR_TILES:
                 prod_of[step - 3] = weigh(act_of[step - 3], step - 3)
+            if ROW_TILES - VECTOR_TILES <= step - 3 < ROW_TILES:
+                prod_of[step - 3] = weigh_on_vector(pre_of[step - 3], step - 3)
             if 0 <= step - 4 < ROW_TILES:
                 j = step - 4
                 sum_experts(prod_of[j], j)

@@ -31,6 +31,7 @@ ROW_TILES = BATCH // P
 STORE_TILES = 8
 X_BUFS = 6
 VECTOR_TILES = 2
+VECTOR_TASKS = 1
 
 FLOPS = 2 * STREAMS * BATCH * FEATURES * COLS
 
@@ -182,38 +183,47 @@ def tile_plelayer_pb_t_e_kernel(
 
         def relu(pre):
             act = work.tile([P, STREAMS, UNITS, EXPERTS], F32)
-            nc.scalar.activation(out=act[:].rearrange("p s v e -> p (s v e)"), in_=pre[:], func=ACT.Relu)
+            nc.scalar.activation(
+                out=act[:, VECTOR_TASKS:].rearrange("p s v e -> p (s v e)"), in_=pre[:, VECTOR_TASKS * COLS :], func=ACT.Relu
+            )
             return act
 
-        def weigh(act, j):
-            shape = [P, TASKS, UNITS, EXPERTS]
+        def weigh_on_vector(prod, pre, j, t, s, first):
+            nc.vector.scalar_tensor_tensor(
+                out=prod[:, t, :, first : first + EXPERTS],
+                in0=pre[:, s * COLS : (s + 1) * COLS].rearrange("p (v e) -> p v e", e=EXPERTS),
+                scalar=0.0,
+                in1=gates[:, t, j, first : first + EXPERTS].unsqueeze(1).to_broadcast([P, UNITS, EXPERTS]),
+                op0=ALU.max,
+                op1=ALU.mult,
+            )
+
+        def weigh(pre, act, j):
             prod = work.tile([P, TASKS, UNITS, GATES], F32)
             nc.gpsimd.tensor_tensor(
-                out=prod[:, :, :, 0:EXPERTS],
-                in0=act[:, 0:TASKS],
-                in1=gates[:, :, j, 0:EXPERTS].unsqueeze(2).to_broadcast(shape),
+                out=prod[:, VECTOR_TASKS:, :, 0:EXPERTS],
+                in0=act[:, VECTOR_TASKS:TASKS],
+                in1=gates[:, VECTOR_TASKS:, j, 0:EXPERTS]
+                .unsqueeze(2)
+                .to_broadcast([P, TASKS - VECTOR_TASKS, UNITS, EXPERTS]),
                 op=ALU.mult,
             )
+            shape = [P, TASKS, UNITS, EXPERTS]
             nc.gpsimd.tensor_tensor(
                 out=prod[:, :, :, EXPERTS:GATES],
                 in0=act[:, TASKS].unsqueeze(1).to_broadcast(shape),
                 in1=gates[:, :, j, EXPERTS:GATES].unsqueeze(2).to_broadcast(shape),
                 op=ALU.mult,
             )
+            for t in range(VECTOR_TASKS):
+                weigh_on_vector(prod, pre, j, t, t, 0)
             return prod
 
-        def weigh_on_vector(pre, j):
+        def weigh_all_on_vector(pre, j):
             prod = work.tile([P, TASKS, UNITS, GATES], F32)
             for t in range(TASKS):
-                for s, first in ((t, 0), (TASKS, EXPERTS)):
-                    nc.vector.scalar_tensor_tensor(
-                        out=prod[:, t, :, first : first + EXPERTS],
-                        in0=pre[:, s * COLS : (s + 1) * COLS].rearrange("p (v e) -> p v e", e=EXPERTS),
-                        scalar=0.0,
-                        in1=gates[:, t, j, first : first + EXPERTS].unsqueeze(1).to_broadcast([P, UNITS, EXPERTS]),
-                        op0=ALU.max,
-                        op1=ALU.mult,
-                    )
+                weigh_on_vector(prod, pre, j, t, t, 0)
+                weigh_on_vector(prod, pre, j, t, TASKS, EXPERTS)
             return prod
 
         def sum_experts(prod, j):
@@ -238,9 +248,9 @@ def tile_plelayer_pb_t_e_kernel(
                 if step - 2 < ROW_TILES - VECTOR_TILES:
                     act_of[step - 2] = relu(pre_of[step - 2])
             if 0 <= step - 3 < ROW_TILES - VECTOR_TILES:
-                prod_of[step - 3] = weigh(act_of[step - 3], step - 3)
+                prod_of[step - 3] = weigh(pre_of[step - 3], act_of[step - 3], step - 3)
             if ROW_TILES - VECTOR_TILES <= step - 3 < ROW_TILES:
-                prod_of[step - 3] = weigh_on_vector(pre_of[step - 3], step - 3)
+                prod_of[step - 3] = weigh_all_on_vector(pre_of[step - 3], step - 3)
             if 0 <= step - 4 < ROW_TILES:
                 j = step - 4
                 sum_experts(prod_of[j], j)

from contextlib import ExitStack

import concourse.mybir as mybir
from concourse.masks import make_identity

F32 = mybir.dt.float32
BF16 = mybir.dt.bfloat16
I32 = mybir.dt.int32
U32 = mybir.dt.uint32
U8 = mybir.dt.uint8
FP8X4 = mybir.dt.float8_e4m3fn_x4
FP4X4 = mybir.dt.float4_e2m1fn_x4
ALU = mybir.AluOpType
ACT = mybir.ActivationFunctionType
AXIS = mybir.AxisListType

P = 128
TASKS = 3
STREAMS = TASKS + 1
BATCH = 4096
FEATURES = 1024
UNITS = 16
EXPERTS = 8
GATES = 2 * EXPERTS
COLS = UNITS * EXPERTS
PACK = 4
K_PASS = P * PACK
PASSES = FEATURES // K_PASS
PAIRS = PACK // 2
ROW_TILES = BATCH // P
STORE_TILES = 8
X_BUFS = 6
VECTOR_TILES = 2
VECTOR_TASKS = 1

FLOPS = 2 * STREAMS * BATCH * FEATURES * COLS


def tile_plelayer_pb_t_e_kernel(
    tc, task_h, share_h, ews1_words, ews1_scales, ebs1, ew1_words, ew1_scales, eb1, gate_pre1, gb1, out
):
    nc = tc.nc
    with ExitStack() as ctx:
        const = ctx.enter_context(tc.tile_pool(name="const", bufs=1))
        x_pool = ctx.enter_context(tc.tile_pool(name="x", bufs=X_BUFS))
        work = ctx.enter_context(tc.tile_pool(name="work", bufs=3))
        turned_pool = ctx.enter_context(tc.psum_pool(name="turned", bufs=6))
        acc_pool = ctx.enter_context(tc.psum_pool(name="acc", bufs=2))
        ctx.enter_context(tc.manual_schedule())

        task_rows = task_h.rearrange("t (p j) k -> p t j k", j=ROW_TILES)
        share_rows = share_h.rearrange("(p j) k -> p j k", j=ROW_TILES)
        out_rows = out.rearrange("t (p j) v -> p t j v", j=ROW_TILES)

        def load_row_tile(j):
            x_tile = x_pool.tile([P, STREAMS, FEATURES], BF16)
            nc.sync.dma_start(out=x_tile[:, 0:TASKS, :], in_=task_rows[:, :, j, :])
            nc.sync.dma_start(out=x_tile[:, TASKS, :], in_=share_rows[:, j, :])
            return x_tile

        x_tiles = {0: load_row_tile(0)}

        w_words = const.tile([P, STREAMS * PASSES, 2 * COLS], U8, align_bytes=64)
        w_planes = const.tile([P, STREAMS * PASSES, COLS], U8, align_bytes=64)
        own_passes = TASKS * PASSES
        nc.vector.memset(w_planes[:].bitcast(I32), 0)
        nc.sync.dma_start(
            out=w_words[:, 0:own_passes, :].bitcast(I32), in_=ew1_words.rearrange("g p n -> p g n").bitcast(I32)
        )
        nc.sync.dma_start(
            out=w_words[:, own_passes:, :].bitcast(I32), in_=ews1_words.rearrange("g p n -> p g n").bitcast(I32)
        )
        for quad in range(4):
            rows = slice(4 * quad, 4 * quad + 4)
            parts = slice(32 * quad, 32 * quad + 4)
            nc.sync.dma_start(
                out=w_planes[parts, 0:own_passes, :].bitcast(I32),
                in_=ew1_scales[:, rows, :].rearrange("g r n -> r g n").bitcast(I32),
            )
            nc.sync.dma_start(
                out=w_planes[parts, own_passes:, :].bitcast(I32),
                in_=ews1_scales[:, rows, :].rearrange("g r n -> r g n").bitcast(I32),
            )

        for j in range(1, X_BUFS):
            x_tiles[j] = load_row_tile(j)

        ident = const.tile([P, P], F32)
        make_identity(nc, ident[:])

        gate_bf = const.tile([P, TASKS, ROW_TILES, GATES], BF16)
        nc.scalar.dma_start(out=gate_bf[:], in_=gate_pre1.rearrange("t (p j) i -> p t j i", j=ROW_TILES))
        gb_bf = const.tile([P, TASKS, GATES], BF16)
        nc.scalar.dma_start(
            out=gb_bf[:].rearrange("p t i -> p (t i)"), in_=gb1.rearrange("t i -> (t i)").partition_broadcast(P)
        )
        bias_bf = const.tile([P, STREAMS * COLS], BF16)
        nc.scalar.dma_start(
            out=bias_bf[:, 0 : TASKS * COLS], in_=eb1.rearrange("t v e -> (t v e)").partition_broadcast(P)
        )
        nc.scalar.dma_start(
            out=bias_bf[:, TASKS * COLS :], in_=ebs1.rearrange("v e -> (v e)").partition_broadcast(P)
        )

        rows_all = TASKS * ROW_TILES
        logits = const.tile([P, TASKS, ROW_TILES, GATES], F32)
        nc.vector.tensor_tensor(
            out=logits[:],
            in0=gate_bf[:],
            in1=gb_bf[:].unsqueeze(2).to_broadcast([P, TASKS, ROW_TILES, GATES]),
            op=ALU.add,
        )
        logits_flat = logits[:].rearrange("p t j i -> p (t j) i")
        top = const.tile([P, rows_all], F32)
        nc.vector.tensor_reduce(out=top[:], in_=logits_flat, axis=AXIS.X, op=ALU.max)
        shifted = const.tile([P, rows_all, GATES], F32)
        nc.vector.tensor_tensor(
            out=shifted[:], in0=logits_flat, in1=top[:].unsqueeze(2).to_broadcast([P, rows_all, GATES]), op=ALU.subtract
        )
        gates = const.tile([P, TASKS, ROW_TILES, GATES], F32)

        def normalise_gates():
            expo = const.tile([P, rows_all, GATES], F32)
            nc.scalar.activation(out=expo[:], in_=shifted[:], func=ACT.Exp)
            total = const.tile([P, rows_all], F32)
            nc.vector.tensor_reduce(out=total[:], in_=expo[:], axis=AXIS.X, op=ALU.add)
            inverse = const.tile([P, rows_all], F32)
            nc.vector.reciprocal(out=inverse[:], in_=total[:])
            nc.gpsimd.tensor_tensor(
                out=gates[:].rearrange("p t j i -> p (t j) i"),
                in0=expo[:],
                in1=inverse[:].unsqueeze(2).to_broadcast([P, rows_all, GATES]),
                op=ALU.mult,
            )

        bias = const.tile([P, STREAMS * COLS], F32)
        nc.vector.tensor_copy(out=bias[:], in_=bias_bf[:])
        result = const.tile([P, TASKS, ROW_TILES, UNITS], F32)

        def transpose_row_tile(x_tile):
            grouped = work.tile([P, STREAMS, PASSES, P, PACK], BF16, align_bytes=64)
            for s in range(STREAMS):
                words = x_tile[:, s, :].bitcast(F32)
                turned = turned_pool.tile([P, PASSES, PAIRS, P], F32)
                for g in range(PASSES):
                    first = g * P * PAIRS
                    for u in range(PAIRS):
                        nc.tensor.transpose(
                            turned[:, g, u, :], words[:, first + u : first + P * PAIRS : PAIRS], ident[:]
                        )
                nc.scalar.copy(out=grouped[:, s].bitcast(F32), in_=turned[:].rearrange("p g u r -> p g r u"))
            return grouped

        def quantise_row_tile(grouped):
            codes = work.tile([P, STREAMS * PASSES * P], U32, align_bytes=64)
            x_scales = work.tile([P, STREAMS * PASSES * P], U8, align_bytes=64)
            nc.vector.quantize_mx(
                out=codes[:].bitcast(FP8X4), scales=x_scales[:], in_=grouped[:].rearrange("p s g r t -> p (s g r t)")
            )
            return codes, x_scales

        def expert_matmuls(codes, x_scales):
            acc = acc_pool.tile([P, STREAMS, COLS], F32)
            for s in range(STREAMS):
                for g in range(PASSES):
                    w = s * PASSES + g
                    rows = slice(w * P, (w + 1) * P)
                    nc.tensor.matmul_mx(
                        out=acc[:, s, :],
                        lhsT=codes[:, rows].bitcast(FP8X4),
                        lhsT_scale=x_scales[:, rows],
                        rhs=w_words[:, w, :].bitcast(FP4X4),
                        rhs_scale=w_planes[:, w, :],
                        start=(g == 0),
                        stop=(g == PASSES - 1),
                    )
            return acc

        def add_bias(acc):
            pre = work.tile([P, STREAMS * COLS], F32)
            nc.vector.tensor_tensor(out=pre[:], in0=acc[:].rearrange("p s n -> p (s n)"), in1=bias[:], op=ALU.add)
            return pre

        def relu(pre):
            act = work.tile([P, STREAMS, UNITS, EXPERTS], F32)
            nc.scalar.activation(
                out=act[:, VECTOR_TASKS:].rearrange("p s v e -> p (s v e)"), in_=pre[:, VECTOR_TASKS * COLS :], func=ACT.Relu
            )
            return act

        def weigh_on_vector(prod, pre, j, t, s, first):
            nc.vector.scalar_tensor_tensor(
                out=prod[:, t, :, first : first + EXPERTS],
                in0=pre[:, s * COLS : (s + 1) * COLS].rearrange("p (v e) -> p v e", e=EXPERTS),
                scalar=0.0,
                in1=gates[:, t, j, first : first + EXPERTS].unsqueeze(1).to_broadcast([P, UNITS, EXPERTS]),
                op0=ALU.max,
                op1=ALU.mult,
            )

        def weigh(pre, act, j):
            prod = work.tile([P, TASKS, UNITS, GATES], F32)
            nc.gpsimd.tensor_tensor(
                out=prod[:, VECTOR_TASKS:, :, 0:EXPERTS],
                in0=act[:, VECTOR_TASKS:TASKS],
                in1=gates[:, VECTOR_TASKS:, j, 0:EXPERTS]
                .unsqueeze(2)
                .to_broadcast([P, TASKS - VECTOR_TASKS, UNITS, EXPERTS]),
                op=ALU.mult,
            )
            shape = [P, TASKS, UNITS, EXPERTS]
            nc.gpsimd.tensor_tensor(
                out=prod[:, :, :, EXPERTS:GATES],
                in0=act[:, TASKS].unsqueeze(1).to_broadcast(shape),
                in1=gates[:, :, j, EXPERTS:GATES].unsqueeze(2).to_broadcast(shape),
                op=ALU.mult,
            )
            for t in range(VECTOR_TASKS):
                weigh_on_vector(prod, pre, j, t, t, 0)
            return prod

        def weigh_all_on_vector(pre, j):
            prod = work.tile([P, TASKS, UNITS, GATES], F32)
            for t in range(TASKS):
                weigh_on_vector(prod, pre, j, t, t, 0)
                weigh_on_vector(prod, pre, j, t, TASKS, EXPERTS)
            return prod

        def sum_experts(prod, j):
            nc.vector.tensor_reduce(out=result[:, :, j, :], in_=prod[:], axis=AXIS.X, op=ALU.add)

        grouped_of = {}
        quantised_of = {}
        acc_of = {}
        pre_of = {}
        act_of = {}
        prod_of = {}
        for step in range(ROW_TILES + 4):
            if step < ROW_TILES:
                grouped_of[step] = transpose_row_tile(x_tiles[step])
                if step + X_BUFS < ROW_TILES:
                    x_tiles[step + X_BUFS] = load_row_tile(step + X_BUFS)
            if 0 <= step - 1 < ROW_TILES:
                codes, x_scales = quantised_of[step - 1]
                acc_of[step - 1] = expert_matmuls(codes, x_scales)
            if 0 <= step - 2 < ROW_TILES:
                pre_of[step - 2] = add_bias(acc_of[step - 2])
                if step - 2 < ROW_TILES - VECTOR_TILES:
                    act_of[step - 2] = relu(pre_of[step - 2])
            if 0 <= step - 3 < ROW_TILES - VECTOR_TILES:
                prod_of[step - 3] = weigh(pre_of[step - 3], act_of[step - 3], step - 3)
            if ROW_TILES - VECTOR_TILES <= step - 3 < ROW_TILES:
                prod_of[step - 3] = weigh_all_on_vector(pre_of[step - 3], step - 3)
            if 0 <= step - 4 < ROW_TILES:
                j = step - 4
                sum_experts(prod_of[j], j)
                if (j + 1) % STORE_TILES == 0:
                    done = slice(j + 1 - STORE_TILES, j + 1)
                    nc.sync.dma_start(out=out_rows[:, :, done, :], in_=result[:, :, done, :])
            if step < ROW_TILES:
                quantised_of[step] = quantise_row_tile(grouped_of[step])
            if step == 0:
                normalise_gates()
